import numpy as np
import ml_dtypes

BF16 = ml_dtypes.bfloat16


def bf(x):
    return np.asarray(x, np.float32).astype(BF16)


def f32(x):
    return np.asarray(x, np.float32)


def f64(x):
    return np.asarray(x).astype(np.float64)


def striped(idx):
    return np.tile(idx.reshape(-1, 16).T, (8, 1))


C, S, B, T, N = 128, 2048, 64, 16, 1024


def setup_inputs():
    return {
        "base": f32(np.random.standard_normal((C, S))),
        "rtgs": f32(np.random.standard_normal((1, N))),
        "ret_w": f32(np.random.standard_normal((C, 1))),
        "ret_b": f32(0.1 * np.random.standard_normal((C, 1))),
        "gp": f32(0.5 * np.random.standard_normal((C, B))),
        "pe": f32(0.5 * np.random.standard_normal((C, T))),
        "offs": striped(np.random.permutation(S)[:N]),
    }


def reference(base, rtgs, ret_w, ret_b, gp, pe, offs):
    idx = offs[:16].T.reshape(-1)
    emb = np.tanh(f64(ret_w) * f64(rtgs) + f64(ret_b))
    pos = (f64(gp)[:, :, None] + f64(pe)[:, None, :]).reshape(C, N)
    out = f64(base).copy()
    out[:, idx] = emb + pos
    return out

@@ -1,0 +1,44 @@
+import concourse.mybir as mybir
+
+C = 128
+S = 2048
+B, T = 64, 16
+N = B * T
+F32, U16 = mybir.dt.float32, mybir.dt.uint16
+ADD = mybir.AluOpType.add
+TANH = mybir.ActivationFunctionType.Tanh
+
+
+def tile_gpt_tit_kernel(tc, base, rtgs, ret_w, ret_b, gp, pe, offs, out):
+    nc = tc.nc
+    with tc.tile_pool(name="held", bufs=1) as held:
+        offsets = held.tile([C, N // 16], U16, name="offsets")
+        nc.sync.dma_start(offsets[:], offs)
+        returns = held.tile([C, N], F32, name="returns")
+        nc.sync.dma_start(returns[:], rtgs.to_broadcast([C, N]))
+        window = held.tile([C, S], F32, name="window")
+        nc.sync.dma_start(window[:], base)
+
+        weight = held.tile([C, 1], F32, name="weight")
+        nc.scalar.dma_start(weight[:], ret_w)
+        bias = held.tile([C, 1], F32, name="bias")
+        nc.scalar.dma_start(bias[:], ret_b)
+        trajectory = held.tile([C, B], F32, name="trajectory")
+        nc.scalar.dma_start(trajectory[:], gp)
+        step = held.tile([C, T], F32, name="step")
+        nc.scalar.dma_start(step[:], pe)
+
+        emb = held.tile([C, N], F32, name="emb")
+        nc.scalar.activation(emb[:], returns[:], TANH, bias=bias[:], scale=weight[:])
+
+        pos = held.tile([C, N], F32, name="pos")
+        nc.vector.tensor_tensor(
+            pos[:].rearrange("c (b t) -> c b t", t=T),
+            trajectory[:].unsqueeze(2).to_broadcast([C, B, T]),
+            step[:].unsqueeze(1).to_broadcast([C, B, T]),
+            ADD,
+        )
+
+        nc.vector.tensor_tensor(window[:].indirect(offsets[:]), emb[:], pos[:], ADD)
+
+        nc.sync.dma_start(out, window[:])

@@ -4,6 +4,8 @@ C = 128
 S = 2048
 B, T = 64, 16
 N = B * T
+BANK = 512
+FLOPS = 2 * 2 * C * N
 F32, U16 = mybir.dt.float32, mybir.dt.uint16
 ADD = mybir.AluOpType.add
 TANH = mybir.ActivationFunctionType.Tanh
@@ -11,25 +13,32 @@ TANH = mybir.ActivationFunctionType.Tanh
 
 def tile_gpt_tit_kernel(tc, base, rtgs, ret_w, ret_b, gp, pe, offs, out):
     nc = tc.nc
-    with tc.tile_pool(name="held", bufs=1) as held:
+    with (
+        tc.tile_pool(name="held", bufs=1) as held,
+        tc.psum_pool(name="psum", bufs=1) as psum,
+    ):
         offsets = held.tile([C, N // 16], U16, name="offsets")
         nc.sync.dma_start(offsets[:], offs)
-        returns = held.tile([C, N], F32, name="returns")
-        nc.sync.dma_start(returns[:], rtgs.to_broadcast([C, N]))
+        moving = held.tile([2, N], F32, name="moving")
+        nc.vector.memset(moving[0:1, :], 1.0)
+        nc.sync.dma_start(moving[1:2, :], rtgs)
         window = held.tile([C, S], F32, name="window")
         nc.sync.dma_start(window[:], base)
 
-        weight = held.tile([C, 1], F32, name="weight")
-        nc.scalar.dma_start(weight[:], ret_w)
-        bias = held.tile([C, 1], F32, name="bias")
-        nc.scalar.dma_start(bias[:], ret_b)
+        affine = held.tile([2, C], F32, name="affine")
+        nc.scalar.dma_start(affine[0:1, :], ret_b.rearrange("c o -> o c"))
+        nc.scalar.dma_start(affine[1:2, :], ret_w.rearrange("c o -> o c"))
         trajectory = held.tile([C, B], F32, name="trajectory")
         nc.scalar.dma_start(trajectory[:], gp)
         step = held.tile([C, T], F32, name="step")
         nc.scalar.dma_start(step[:], pe)
 
         emb = held.tile([C, N], F32, name="emb")
-        nc.scalar.activation(emb[:], returns[:], TANH, bias=bias[:], scale=weight[:])
+        for k in range(N // BANK):
+            columns = slice(k * BANK, (k + 1) * BANK)
+            argument = psum.tile([C, BANK], F32, name=f"argument{k}")
+            nc.tensor.matmul(argument[:], affine[:], moving[:, columns], start=True, stop=True)
+            nc.scalar.activation(emb[:, columns], argument[:], TANH)
 
         pos = held.tile([C, N], F32, name="pos")
         nc.vector.tensor_tensor(

@@ -5,8 +5,9 @@ S = 2048
 B, T = 64, 16
 N = B * T
 BANK = 512
+WARMING = 4
 FLOPS = 2 * 2 * C * N
-F32, U16 = mybir.dt.float32, mybir.dt.uint16
+F32, BF16, U16 = mybir.dt.float32, mybir.dt.bfloat16, mybir.dt.uint16
 ADD = mybir.AluOpType.add
 TANH = mybir.ActivationFunctionType.Tanh
 
@@ -17,6 +18,12 @@ def tile_gpt_tit_kernel(tc, base, rtgs, ret_w, ret_b, gp, pe, offs, out):
         tc.tile_pool(name="held", bufs=1) as held,
         tc.psum_pool(name="psum", bufs=1) as psum,
     ):
+        zeros = held.tile([C, BANK], BF16, name="zeros")
+        nc.vector.memset(zeros[:], 0.0)
+        unused = psum.tile([C, BANK], F32, name="unused")
+        for repeat in range(WARMING):
+            nc.tensor.matmul(unused[:], zeros[:, 0:C], zeros[:], start=True, stop=True)
+
         offsets = held.tile([C, N // 16], U16, name="offsets")
         nc.sync.dma_start(offsets[:], offs)
         moving = held.tile([2, N], F32, name="moving")

@@ -5,6 +5,7 @@ S = 2048
 B, T = 64, 16
 N = B * T
 BANK = 512
+PIECE = 256
 WARMING = 4
 FLOPS = 2 * 2 * C * N
 F32, BF16, U16 = mybir.dt.float32, mybir.dt.bfloat16, mybir.dt.uint16
@@ -41,9 +42,9 @@ def tile_gpt_tit_kernel(tc, base, rtgs, ret_w, ret_b, gp, pe, offs, out):
         nc.scalar.dma_start(step[:], pe)
 
         emb = held.tile([C, N], F32, name="emb")
-        for k in range(N // BANK):
-            columns = slice(k * BANK, (k + 1) * BANK)
-            argument = psum.tile([C, BANK], F32, name=f"argument{k}")
+        for k in range(N // PIECE):
+            columns = slice(k * PIECE, (k + 1) * PIECE)
+            argument = psum.tile([C, PIECE], F32, name=f"argument{k}")
             nc.tensor.matmul(argument[:], affine[:], moving[:, columns], start=True, stop=True)
             nc.scalar.activation(emb[:, columns], argument[:], TANH)
 

@@ -30,16 +30,16 @@ def tile_gpt_tit_kernel(tc, base, rtgs, ret_w, ret_b, gp, pe, offs, out):
         moving = held.tile([2, N], F32, name="moving")
         nc.vector.memset(moving[0:1, :], 1.0)
         nc.sync.dma_start(moving[1:2, :], rtgs)
+        trajectory = held.tile([C, B], F32, name="trajectory")
+        nc.sync.dma_start(trajectory[:], gp)
+        step = held.tile([C, T], F32, name="step")
+        nc.sync.dma_start(step[:], pe)
         window = held.tile([C, S], F32, name="window")
         nc.sync.dma_start(window[:], base)
 
         affine = held.tile([2, C], F32, name="affine")
         nc.scalar.dma_start(affine[0:1, :], ret_b.rearrange("c o -> o c"))
         nc.scalar.dma_start(affine[1:2, :], ret_w.rearrange("c o -> o c"))
-        trajectory = held.tile([C, B], F32, name="trajectory")
-        nc.scalar.dma_start(trajectory[:], gp)
-        step = held.tile([C, T], F32, name="step")
-        nc.scalar.dma_start(step[:], pe)
 
         emb = held.tile([C, N], F32, name="emb")
         for k in range(N // PIECE):

@@ -5,7 +5,7 @@ S = 2048
 B, T = 64, 16
 N = B * T
 BANK = 512
-PIECE = 256
+PIECES = (512, 256, 128, 128)
 WARMING = 4
 FLOPS = 2 * 2 * C * N
 F32, BF16, U16 = mybir.dt.float32, mybir.dt.bfloat16, mybir.dt.uint16
@@ -19,11 +19,17 @@ def tile_gpt_tit_kernel(tc, base, rtgs, ret_w, ret_b, gp, pe, offs, out):
         tc.tile_pool(name="held", bufs=1) as held,
         tc.psum_pool(name="psum", bufs=1) as psum,
     ):
-        zeros = held.tile([C, BANK], BF16, name="zeros")
+        zeros = held.tile([C, C], BF16, name="zeros")
         nc.vector.memset(zeros[:], 0.0)
         unused = psum.tile([C, BANK], F32, name="unused")
         for repeat in range(WARMING):
-            nc.tensor.matmul(unused[:], zeros[:, 0:C], zeros[:], start=True, stop=True)
+            nc.tensor.matmul(
+                unused[:].rearrange("c (r n) -> c r n", n=C),
+                zeros[:],
+                zeros[:].unsqueeze(1).to_broadcast([C, BANK // C, C]),
+                start=True,
+                stop=True,
+            )
 
         offsets = held.tile([C, N // 16], U16, name="offsets")
         nc.sync.dma_start(offsets[:], offs)
@@ -42,9 +48,10 @@ def tile_gpt_tit_kernel(tc, base, rtgs, ret_w, ret_b, gp, pe, offs, out):
         nc.scalar.dma_start(affine[1:2, :], ret_w.rearrange("c o -> o c"))
 
         emb = held.tile([C, N], F32, name="emb")
-        for k in range(N // PIECE):
-            columns = slice(k * PIECE, (k + 1) * PIECE)
-            argument = psum.tile([C, PIECE], F32, name=f"argument{k}")
+        for k, width in enumerate(PIECES):
+            first = sum(PIECES[:k])
+            columns = slice(first, first + width)
+            argument = psum.tile([C, width], F32, name=f"argument{k}")
             nc.tensor.matmul(argument[:], affine[:], moving[:, columns], start=True, stop=True)
             nc.scalar.activation(emb[:, columns], argument[:], TANH)
 

@@ -1,14 +1,15 @@
 import concourse.mybir as mybir
+from concourse.masks import make_identity
 
 C = 128
 S = 2048
 B, T = 64, 16
 N = B * T
 BANK = 512
-PIECES = (512, 256, 128, 128)
-WARMING = 4
-FLOPS = 2 * 2 * C * N
-F32, BF16, U16 = mybir.dt.float32, mybir.dt.bfloat16, mybir.dt.uint16
+HALVES = N // BANK
+Q = BANK // C
+FLOPS = 2 * C * N
+F32, U16 = mybir.dt.float32, mybir.dt.uint16
 ADD = mybir.AluOpType.add
 TANH = mybir.ActivationFunctionType.Tanh
 
@@ -19,41 +20,44 @@ def tile_gpt_tit_kernel(tc, base, rtgs, ret_w, ret_b, gp, pe, offs, out):
         tc.tile_pool(name="held", bufs=1) as held,
         tc.psum_pool(name="psum", bufs=1) as psum,
     ):
-        zeros = held.tile([C, C], BF16, name="zeros")
-        nc.vector.memset(zeros[:], 0.0)
-        unused = psum.tile([C, BANK], F32, name="unused")
-        for repeat in range(WARMING):
-            nc.tensor.matmul(
-                unused[:].rearrange("c (r n) -> c r n", n=C),
-                zeros[:],
-                zeros[:].unsqueeze(1).to_broadcast([C, BANK // C, C]),
-                start=True,
-                stop=True,
-            )
-
-        offsets = held.tile([C, N // 16], U16, name="offsets")
-        nc.sync.dma_start(offsets[:], offs)
-        moving = held.tile([2, N], F32, name="moving")
-        nc.vector.memset(moving[0:1, :], 1.0)
-        nc.sync.dma_start(moving[1:2, :], rtgs)
+        returns = held.tile([C, HALVES, Q], F32, name="returns")
+        nc.sync.dma_start(returns[:], rtgs.rearrange("o (h k q) -> k (o h) q", h=HALVES, q=Q))
         trajectory = held.tile([C, B], F32, name="trajectory")
         nc.sync.dma_start(trajectory[:], gp)
         step = held.tile([C, T], F32, name="step")
         nc.sync.dma_start(step[:], pe)
+        offsets = held.tile([C, N // 16], U16, name="offsets")
+        nc.sync.dma_start(offsets[:], offs)
         window = held.tile([C, S], F32, name="window")
         nc.sync.dma_start(window[:], base)
 
-        affine = held.tile([2, C], F32, name="affine")
-        nc.scalar.dma_start(affine[0:1, :], ret_b.rearrange("c o -> o c"))
-        nc.scalar.dma_start(affine[1:2, :], ret_w.rearrange("c o -> o c"))
+        weight = held.tile([C, 1], F32, name="weight")
+        nc.scalar.dma_start(weight[:], ret_w)
+        bias = held.tile([C, 1], F32, name="bias")
+        nc.scalar.dma_start(bias[:], ret_b)
+
+        warm = held.tile([C, 1], F32, name="warm")
+        nc.vector.memset(warm[:], 0.0)
+        warmed = held.tile([C, 1], F32, name="warmed")
+        nc.scalar.activation(warmed[:], warm[:], TANH)
+
+        identity = held.tile([C, C], F32, name="identity")
+        make_identity(nc, identity[:])
 
         emb = held.tile([C, N], F32, name="emb")
-        for k, width in enumerate(PIECES):
-            first = sum(PIECES[:k])
-            columns = slice(first, first + width)
-            argument = psum.tile([C, width], F32, name=f"argument{k}")
-            nc.tensor.matmul(argument[:], affine[:], moving[:, columns], start=True, stop=True)
-            nc.scalar.activation(emb[:, columns], argument[:], TANH)
+        for h in range(HALVES):
+            spread = psum.tile([C, Q, C], F32, name=f"spread{h}")
+            for q in range(Q):
+                nc.tensor.transpose(
+                    spread[:, q, :], returns[:, h, q : q + 1].to_broadcast([C, C]), identity[:]
+                )
+            nc.scalar.activation(
+                emb[:, h * BANK : (h + 1) * BANK].rearrange("c (k q) -> c k q", q=Q),
+                spread[:].rearrange("c q k -> c k q"),
+                TANH,
+                bias=bias[:],
+                scale=weight[:],
+            )
 
         pos = held.tile([C, N], F32, name="pos")
         nc.vector.tensor_tensor(

@@ -6,7 +6,7 @@ S = 2048
 B, T = 64, 16
 N = B * T
 BANK = 512
-HALVES = N // BANK
+RUN = N // C
 Q = BANK // C
 FLOPS = 2 * C * N
 F32, U16 = mybir.dt.float32, mybir.dt.uint16
@@ -20,8 +20,8 @@ def tile_gpt_tit_kernel(tc, base, rtgs, ret_w, ret_b, gp, pe, offs, out):
         tc.tile_pool(name="held", bufs=1) as held,
         tc.psum_pool(name="psum", bufs=1) as psum,
     ):
-        returns = held.tile([C, HALVES, Q], F32, name="returns")
-        nc.sync.dma_start(returns[:], rtgs.rearrange("o (h k q) -> k (o h) q", h=HALVES, q=Q))
+        returns = held.tile([C, RUN], F32, name="returns")
+        nc.sync.dma_start(returns[:], rtgs.rearrange("o (k i) -> (o k) i", i=RUN))
         trajectory = held.tile([C, B], F32, name="trajectory")
         nc.sync.dma_start(trajectory[:], gp)
         step = held.tile([C, T], F32, name="step")
@@ -45,14 +45,14 @@ def tile_gpt_tit_kernel(tc, base, rtgs, ret_w, ret_b, gp, pe, offs, out):
         make_identity(nc, identity[:])
 
         emb = held.tile([C, N], F32, name="emb")
-        for h in range(HALVES):
-            spread = psum.tile([C, Q, C], F32, name=f"spread{h}")
+        emb_runs = emb[:].rearrange("c (k i) -> c k i", i=RUN)
+        for first in range(0, RUN, Q):
+            spread = psum.tile([C, Q, C], F32, name=f"spread{first}")
             for q in range(Q):
-                nc.tensor.transpose(
-                    spread[:, q, :], returns[:, h, q : q + 1].to_broadcast([C, C]), identity[:]
-                )
+                column = returns[:, first + q : first + q + 1]
+                nc.tensor.transpose(spread[:, q, :], column.to_broadcast([C, C]), identity[:])
             nc.scalar.activation(
-                emb[:, h * BANK : (h + 1) * BANK].rearrange("c (k q) -> c k q", q=Q),
+                emb_runs[:, :, first : first + Q],
                 spread[:].rearrange("c q k -> c k q"),
                 TANH,
                 bias=bias[:],

import concourse.mybir as mybir
from concourse.masks import make_identity

C = 128
S = 2048
B, T = 64, 16
N = B * T
BANK = 512
RUN = N // C
Q = BANK // C
FLOPS = 2 * C * N
F32, U16 = mybir.dt.float32, mybir.dt.uint16
ADD = mybir.AluOpType.add
TANH = mybir.ActivationFunctionType.Tanh


def tile_gpt_tit_kernel(tc, base, rtgs, ret_w, ret_b, gp, pe, offs, out):
    nc = tc.nc
    with (
        tc.tile_pool(name="held", bufs=1) as held,
        tc.psum_pool(name="psum", bufs=1) as psum,
    ):
        returns = held.tile([C, RUN], F32, name="returns")
        nc.sync.dma_start(returns[:], rtgs.rearrange("o (k i) -> (o k) i", i=RUN))
        trajectory = held.tile([C, B], F32, name="trajectory")
        nc.sync.dma_start(trajectory[:], gp)
        step = held.tile([C, T], F32, name="step")
        nc.sync.dma_start(step[:], pe)
        offsets = held.tile([C, N // 16], U16, name="offsets")
        nc.sync.dma_start(offsets[:], offs)
        window = held.tile([C, S], F32, name="window")
        nc.sync.dma_start(window[:], base)

        weight = held.tile([C, 1], F32, name="weight")
        nc.scalar.dma_start(weight[:], ret_w)
        bias = held.tile([C, 1], F32, name="bias")
        nc.scalar.dma_start(bias[:], ret_b)

        warm = held.tile([C, 1], F32, name="warm")
        nc.vector.memset(warm[:], 0.0)
        warmed = held.tile([C, 1], F32, name="warmed")
        nc.scalar.activation(warmed[:], warm[:], TANH)

        identity = held.tile([C, C], F32, name="identity")
        make_identity(nc, identity[:])

        emb = held.tile([C, N], F32, name="emb")
        emb_runs = emb[:].rearrange("c (k i) -> c k i", i=RUN)
        for first in range(0, RUN, Q):
            spread = psum.tile([C, Q, C], F32, name=f"spread{first}")
            for q in range(Q):
                column = returns[:, first + q : first + q + 1]
                nc.tensor.transpose(spread[:, q, :], column.to_broadcast([C, C]), identity[:])
            nc.scalar.activation(
                emb_runs[:, :, first : first + Q],
                spread[:].rearrange("c q k -> c k q"),
                TANH,
                bias=bias[:],
                scale=weight[:],
            )

        pos = held.tile([C, N], F32, name="pos")
        nc.vector.tensor_tensor(
            pos[:].rearrange("c (b t) -> c b t", t=T),
            trajectory[:].unsqueeze(2).to_broadcast([C, B, T]),
            step[:].unsqueeze(1).to_broadcast([C, B, T]),
            ADD,
        )

        nc.vector.tensor_tensor(window[:].indirect(offsets[:]), emb[:], pos[:], ADD)

        nc.sync.dma_start(out, window[:])
